import numpy as np
import ml_dtypes


def mxq(x, axis, fmt="e4m3"):
    dtype, down = {"e4m3": (ml_dtypes.float8_e4m3fn, 7), "e5m2": (ml_dtypes.float8_e5m2, 14)}[fmt]
    v = np.moveaxis(np.asarray(x, np.float32).astype(ml_dtypes.bfloat16).astype(np.float64), axis, -1)
    blocks = v.reshape(v.shape[:-1] + (-1, 32))
    amax = np.abs(blocks).max(-1, keepdims=True)
    byte = np.maximum(np.where(amax > 0, np.frexp(amax)[1] - 1 + 127, 0) - down, 1)
    scale = np.exp2(byte - 127.0)
    codes = (blocks / scale).astype(np.float32).astype(dtype).astype(np.float64)
    return np.moveaxis((codes * scale).reshape(v.shape), -1, axis)


WIDE = False


def mx_kscale(k):
    if not WIDE:
        return np.ones(k)
    levels = np.array([10, -10, 5, -5, 0])
    a = np.random.permutation(np.resize(levels, k // 512 * 4)).reshape(k // 512, 4)
    idx = np.arange(k)
    return np.exp2(a[idx // 512, idx % 128 // 32])


BF16 = ml_dtypes.bfloat16


def bf(x):
    return np.asarray(x, np.float32).astype(BF16)


def f64(x):
    return np.asarray(x).astype(np.float64)


B, N1, N2, D, H, E = 32, 15, 17, 1024, 2, 64
N = N1 * N2 + 1
NDIMS = 2
KMAX = E // (2 * NDIMS)
BASE = 10000.0
PMAX = 3.0


def rope2d(xh, pos0, pos1):
    theta = 1.0 / (BASE ** (np.arange(KMAX) / KMAX))
    ang0 = np.broadcast_to(pos0[:, :, None, None] * theta, (B, N1, N2, KMAX))
    ang1 = np.broadcast_to(pos1[:, None, :, None] * theta, (B, N1, N2, KMAX))
    ang = np.concatenate([ang0, ang1], axis=-1).reshape(B, N - 1, 1, E // 2)
    cos, sin = np.cos(ang), np.sin(ang)
    t = xh[:, 1:]
    tr, ti = t[..., 0::2], t[..., 1::2]
    rr = tr * cos - ti * sin
    ri = tr * sin + ti * cos
    rot = np.stack([rr, ri], axis=-1).reshape(B, N - 1, H, E)
    return np.concatenate([xh[:, :1], rot], axis=1)


def setup_inputs():
    s = mx_kscale(D)
    return {"x": bf(np.random.standard_normal((B, N, D)) * s),
            "pos0": bf(np.random.uniform(-1.0, 1.0, (B, N1)) * PMAX),
            "pos1": bf(np.random.uniform(-1.0, 1.0, (B, N2)) * PMAX),
            "wq": bf(np.random.standard_normal((H * E, D)) * 1.5 / np.sqrt(D) / s),
            "wk": bf(np.random.standard_normal((H * E, D)) * 1.5 / np.sqrt(D) / s)}


def reference(x, pos0, pos1, wq, wk):
    xq = mxq(f64(x), 2, "e4m3")
    q = (xq @ mxq(f64(wq), 1, "e4m3").T).reshape(B, N, H, E)
    k = (xq @ mxq(f64(wk), 1, "e4m3").T).reshape(B, N, H, E)
    p0, p1 = f64(pos0), f64(pos1)
    return rope2d(q, p0, p1), rope2d(k, p0, p1)

@@ -1,0 +1,242 @@
+from contextlib import ExitStack
+
+import concourse.mybir as mybir
+from concourse.masks import make_identity
+
+F32 = mybir.dt.float32
+BF16 = mybir.dt.bfloat16
+U32 = mybir.dt.uint32
+U8 = mybir.dt.uint8
+FP8X4 = mybir.dt.float8_e4m3fn_x4
+ALU = mybir.AluOpType
+ACT = mybir.ActivationFunctionType
+
+P = 128
+BATCH, ROWS, COLS = 32, 15, 17
+TOKENS = 256
+DIM = 1024
+HEADS, PAIRS = 2, 32
+FEATURES = HEADS * PAIRS * 2
+FREQS = PAIRS // 2
+BASE = 10000.0
+
+QUARTERS = P // BATCH
+TILES = TOKENS // QUARTERS
+PACK = 4
+PASSES = DIM // (P * PACK)
+WORD_TILES = DIM // (2 * P)
+STEP_TILES = 4
+STEPS = TILES // STEP_TILES
+BANK_TILES = 2
+STEP_BANKS = STEP_TILES // BANK_TILES
+LOADS_AHEAD = 7
+TRIG_STEPS = 4
+TRIG_TILES = TRIG_STEPS * STEP_TILES
+
+FLOPS = 2 * BATCH * TOKENS * DIM * 2 * FEATURES
+
+
+def transpose_rows(nc, psum, rows, identity):
+    words = rows.bitcast(F32)
+    flipped = psum.tile([P, WORD_TILES, P], F32)
+    for w in range(WORD_TILES):
+        nc.tensor.transpose(flipped[:, w, :], words[:, w * P : (w + 1) * P], identity)
+    return flipped
+
+
+def group_pairs(nc, grouped, flipped):
+    nc.scalar.copy(
+        out=grouped.bitcast(F32),
+        in_=flipped[:].rearrange("p (g u) r -> p g r u", u=2),
+    )
+
+
+def tile_attention_pa_t_kernel(tc, x, pos0, pos1, wq, wk, out_0, out_1):
+    nc = tc.nc
+    x_view = x.rearrange("b (r t) k -> (b r) t k", t=TILES)
+    out_views = [o.rearrange("b (r t) h f -> (b r) t (h f)", t=TILES) for o in (out_0, out_1)]
+
+    with ExitStack() as ctx:
+        const = ctx.enter_context(tc.tile_pool(name="const", bufs=1))
+        x_pool = ctx.enter_context(tc.tile_pool(name="x_rows", bufs=LOADS_AHEAD + 1))
+        work = ctx.enter_context(tc.tile_pool(name="work", bufs=3))
+        flip_psum = ctx.enter_context(tc.psum_pool(name="flip_psum", bufs=4))
+
+        w_rows = const.tile([P, 2, DIM], BF16)
+        nc.sync.dma_start(out=w_rows[:, 0, :], in_=wq)
+        nc.sync.dma_start(out=w_rows[:, 1, :], in_=wk)
+
+        x_rows = {}
+
+        def load(step):
+            rows = x_pool.tile([P, STEP_TILES, DIM], BF16, name="rows")
+            nc.sync.dma_start(out=rows[:], in_=x_view[:, step * STEP_TILES : (step + 1) * STEP_TILES, :])
+            x_rows[step] = rows
+
+        for step in range(LOADS_AHEAD):
+            load(step)
+
+        pos0_rows = const.tile([P, ROWS], BF16)
+        pos1_rows = const.tile([P, COLS], BF16)
+        nc.vector.memset(pos0_rows[:], 0.0)
+        nc.vector.memset(pos1_rows[:], 0.0)
+        nc.scalar.dma_start(out=pos0_rows[0:BATCH, :], in_=pos0)
+        nc.scalar.dma_start(out=pos1_rows[0:BATCH, :], in_=pos1)
+
+        ones = const.tile([P, 1], F32)
+        nc.vector.memset(ones[:], 1.0)
+        first_sin = const.tile([P, 1], F32)
+        nc.scalar.activation(out=first_sin[:], in_=ones[:], func=ACT.Sin)
+
+        identity = const.tile([P, P], F32)
+        make_identity(nc, identity[:])
+
+        w_grouped = const.tile([P, PASSES, 2, P, PACK], BF16, align_bytes=64)
+        for which in range(2):
+            flipped = transpose_rows(nc, flip_psum, w_rows[:, which, :], identity[:])
+            group_pairs(nc, w_grouped[:, :, which, :, :], flipped)
+        w_codes = const.tile([P, PASSES, 2 * P], U32, align_bytes=64)
+        w_scales = const.tile([P, PASSES, 2 * P], U8, align_bytes=64)
+        nc.vector.quantize_mx(
+            out=w_codes[:].rearrange("p g n -> p (g n)").bitcast(FP8X4),
+            scales=w_scales[:].rearrange("p g n -> p (g n)"),
+            in_=w_grouped[:].rearrange("p g w n j -> p (g w n j)"),
+        )
+
+        coords = const.tile([P, 2, TOKENS], BF16)
+        nc.vector.memset(coords[:, :, 0:1], 0.0)
+        nc.vector.tensor_copy(
+            out=coords[:, 0, 1:TOKENS].rearrange("b (i j) -> b i j", j=COLS),
+            in_=pos0_rows[:].unsqueeze(2).to_broadcast([P, ROWS, COLS]),
+        )
+        nc.vector.tensor_copy(
+            out=coords[:, 1, 1:TOKENS].rearrange("b (i j) -> b i j", j=COLS),
+            in_=pos1_rows[:].unsqueeze(1).to_broadcast([P, ROWS, COLS]),
+        )
+        send = const.tile([P, QUARTERS, BATCH, QUARTERS], BF16)
+        nc.vector.memset(send[:], 0.0)
+        for r in range(QUARTERS):
+            nc.vector.tensor_copy(out=send[:, r, :, r], in_=identity[:, 0:BATCH])
+        own_coords = const.tile([P, 2, TILES], F32)
+        with tc.psum_pool(name="coord_psum", bufs=1) as coord_psum:
+            sent = coord_psum.tile([P, 2, TILES], F32)
+            for axis in range(2):
+                for r in range(QUARTERS):
+                    nc.tensor.matmul(
+                        out=sent[:, axis, :],
+                        lhsT=send[:, r, :, :].rearrange("k b q -> k (b q)"),
+                        rhs=coords[:, axis, r * TILES : (r + 1) * TILES],
+                        start=(r == 0),
+                        stop=(r == QUARTERS - 1),
+                    )
+            nc.vector.tensor_copy(out=own_coords[:], in_=sent[:])
+        prod_psum = ctx.enter_context(tc.psum_pool(name="prod_psum", bufs=2 * STEP_BANKS))
+        theta = const.tile([P, FREQS], F32)
+        for m in range(FREQS):
+            nc.vector.tensor_scalar(
+                out=theta[:, m : m + 1], in0=ones[:], scalar1=1.0 / BASE ** (m / FREQS), scalar2=None, op0=ALU.mult
+            )
+        angle = const.tile([P, TILES, 2, FREQS], F32)
+        nc.vector.tensor_tensor(
+            out=angle[:],
+            in0=own_coords[:].rearrange("p a t -> p t a").unsqueeze(3).to_broadcast([P, TILES, 2, FREQS]),
+            in1=theta[:].unsqueeze(1).unsqueeze(2).to_broadcast([P, TILES, 2, FREQS]),
+            op=ALU.mult,
+        )
+        trig = const.tile([P, TILES, 3, PAIRS], F32)
+
+        def build_trig(part):
+            tiles = slice(part * TRIG_TILES, (part + 1) * TRIG_TILES)
+            angle_pairs = angle[:, tiles].rearrange("p t a m -> p t (a m)")
+            half_sin = work.tile([P, TRIG_TILES, PAIRS], F32, name="half_sin")
+            half_sin_sq = work.tile([P, TRIG_TILES, PAIRS], F32, name="half_sin_sq")
+            nc.scalar.activation(out=half_sin[:], in_=angle_pairs, func=ACT.Sin, scale=0.5)
+            nc.scalar.activation(out=half_sin_sq[:], in_=half_sin[:], func=ACT.Square)
+            nc.scalar.activation(out=trig[:, tiles, 2, :], in_=angle_pairs, func=ACT.Sin)
+            nc.scalar.activation(out=trig[:, tiles, 0, :], in_=angle_pairs, func=ACT.Sin, scale=-1.0)
+            nc.vector.tensor_scalar(
+                out=trig[:, tiles, 1, :], in0=half_sin_sq[:], scalar1=-2.0, scalar2=1.0, op0=ALU.mult, op1=ALU.add
+            )
+
+        build_trig(0)
+
+        grouped_rows = {}
+        quantised = {}
+        products = {}
+
+        def transpose_and_group(step):
+            grouped = work.tile([P, STEP_TILES, PASSES, P, PACK], BF16, align_bytes=64, name="grouped")
+            for i in range(STEP_TILES):
+                flipped = transpose_rows(nc, flip_psum, x_rows[step][:, i, :], identity[:])
+                group_pairs(nc, grouped[:, i], flipped)
+            grouped_rows[step] = grouped
+
+        def quantise(step):
+            codes = work.tile([P, STEP_TILES, PASSES, P], U32, align_bytes=64, name="codes")
+            scales = work.tile([P, STEP_TILES, PASSES, P], U8, align_bytes=64, name="scales")
+            nc.vector.quantize_mx(
+                out=codes[:].rearrange("p t g r -> p (t g r)").bitcast(FP8X4),
+                scales=scales[:].rearrange("p t g r -> p (t g r)"),
+                in_=grouped_rows[step][:].rearrange("p t g r j -> p (t g r j)"),
+            )
+            quantised[step] = (codes, scales)
+
+        def project(step):
+            codes, scales = quantised[step]
+            products[step] = []
+            for bank in range(STEP_BANKS):
+                product = prod_psum.tile([P, BANK_TILES, 2 * HEADS, PAIRS, 2], F32, name="product")
+                for j in range(BANK_TILES):
+                    i = bank * BANK_TILES + j
+                    for g in range(PASSES):
+                        nc.tensor.matmul_mx(
+                            out=product[:, j].rearrange("p c r e -> p (c r e)"),
+                            lhsT=codes[:, i, g, :].bitcast(FP8X4),
+                            lhsT_scale=scales[:, i, g, :],
+                            rhs=w_codes[:, g, :].bitcast(FP8X4),
+                            rhs_scale=w_scales[:, g, :],
+                            start=(g == 0),
+                            stop=(g == PASSES - 1),
+                        )
+                products[step].append(product)
+
+        def rotate_and_store(step):
+            spread = [P, 2 * HEADS, PAIRS, 2]
+            from_re = work.tile([P, STEP_TILES] + spread[1:], F32, name="from_re")
+            from_im = work.tile([P, STEP_TILES] + spread[1:], F32, name="from_im")
+            for i in range(STEP_TILES):
+                product = products[step][i // BANK_TILES][:, i % BANK_TILES]
+                t = step * STEP_TILES + i
+                for part, result, low_row in ((0, from_re, 1), (1, from_im, 0)):
+                    nc.vector.tensor_tensor(
+                        out=result[:, i],
+                        in0=product[:, :, :, part : part + 1].to_broadcast(spread),
+                        in1=trig[:, t, low_row : low_row + 2, :].rearrange("p e r -> p r e").unsqueeze(1).to_broadcast(spread),
+                        op=ALU.mult,
+                    )
+            rotated = work.tile([P, 2, STEP_TILES, FEATURES], F32, name="rotated")
+            nc.gpsimd.tensor_tensor(
+                out=rotated[:].rearrange("p w t f -> p t w f"),
+                in0=from_re[:].rearrange("p t (w h) r e -> p t w (h r e)", w=2),
+                in1=from_im[:].rearrange("p t (w h) r e -> p t w (h r e)", w=2),
+                op=ALU.add,
+            )
+            for which in range(2):
+                nc.sync.dma_start(
+                    out=out_views[which][:, step * STEP_TILES : (step + 1) * STEP_TILES, :],
+                    in_=rotated[:, which],
+                )
+
+        for step in range(STEPS + 2):
+            if step + LOADS_AHEAD < STEPS:
+                load(step + LOADS_AHEAD)
+            if step < STEPS:
+                transpose_and_group(step)
+            if 1 <= step <= STEPS:
+                project(step - 1)
+            if step >= 2:
+                rotate_and_store(step - 2)
+            if step < STEPS:
+                quantise(step)
+            if step % TRIG_STEPS == 0 and step + TRIG_STEPS < STEPS:
+                build_trig(step // TRIG_STEPS + 1)

@@ -17,6 +17,7 @@ TOKENS = 256
 DIM = 1024
 HEADS, PAIRS = 2, 32
 FEATURES = HEADS * PAIRS * 2
+SETS = 2 * HEADS
 FREQS = PAIRS // 2
 BASE = 10000.0
 
@@ -63,8 +64,12 @@ def tile_attention_pa_t_kernel(tc, x, pos0, pos1, wq, wk, out_0, out_1):
         flip_psum = ctx.enter_context(tc.psum_pool(name="flip_psum", bufs=4))
 
         w_rows = const.tile([P, 2, DIM], BF16)
-        nc.sync.dma_start(out=w_rows[:, 0, :], in_=wq)
-        nc.sync.dma_start(out=w_rows[:, 1, :], in_=wk)
+        for which, w in enumerate((wq, wk)):
+            for h in range(HEADS):
+                nc.sync.dma_start(
+                    out=w_rows[which * HEADS + h : P : SETS, :, :],
+                    in_=w[h * 2 * PAIRS : (h + 1) * 2 * PAIRS, :].rearrange("(a j) k -> j a k", a=2),
+                )
 
         x_rows = {}
 
@@ -92,9 +97,9 @@ def tile_attention_pa_t_kernel(tc, x, pos0, pos1, wq, wk, out_0, out_1):
         make_identity(nc, identity[:])
 
         w_grouped = const.tile([P, PASSES, 2, P, PACK], BF16, align_bytes=64)
-        for which in range(2):
-            flipped = transpose_rows(nc, flip_psum, w_rows[:, which, :], identity[:])
-            group_pairs(nc, w_grouped[:, :, which, :, :], flipped)
+        for half in range(2):
+            flipped = transpose_rows(nc, flip_psum, w_rows[:, half, :], identity[:])
+            group_pairs(nc, w_grouped[:, :, half, :, :], flipped)
         w_codes = const.tile([P, PASSES, 2 * P], U32, align_bytes=64)
         w_scales = const.tile([P, PASSES, 2 * P], U8, align_bytes=64)
         nc.vector.quantize_mx(
@@ -143,7 +148,7 @@ def tile_attention_pa_t_kernel(tc, x, pos0, pos1, wq, wk, out_0, out_1):
             in1=theta[:].unsqueeze(1).unsqueeze(2).to_broadcast([P, TILES, 2, FREQS]),
             op=ALU.mult,
         )
-        trig = const.tile([P, TILES, 3, PAIRS], F32)
+        trig = const.tile([P, 3, TILES, PAIRS], F32)
 
         def build_trig(part):
             tiles = slice(part * TRIG_TILES, (part + 1) * TRIG_TILES)
@@ -152,10 +157,10 @@ def tile_attention_pa_t_kernel(tc, x, pos0, pos1, wq, wk, out_0, out_1):
             half_sin_sq = work.tile([P, TRIG_TILES, PAIRS], F32, name="half_sin_sq")
             nc.scalar.activation(out=half_sin[:], in_=angle_pairs, func=ACT.Sin, scale=0.5)
             nc.scalar.activation(out=half_sin_sq[:], in_=half_sin[:], func=ACT.Square)
-            nc.scalar.activation(out=trig[:, tiles, 2, :], in_=angle_pairs, func=ACT.Sin)
-            nc.scalar.activation(out=trig[:, tiles, 0, :], in_=angle_pairs, func=ACT.Sin, scale=-1.0)
+            nc.scalar.activation(out=trig[:, 2, tiles, :], in_=angle_pairs, func=ACT.Sin)
+            nc.scalar.activation(out=trig[:, 0, tiles, :], in_=angle_pairs, func=ACT.Sin, scale=-1.0)
             nc.vector.tensor_scalar(
-                out=trig[:, tiles, 1, :], in0=half_sin_sq[:], scalar1=-2.0, scalar2=1.0, op0=ALU.mult, op1=ALU.add
+                out=trig[:, 1, tiles, :], in0=half_sin_sq[:], scalar1=-2.0, scalar2=1.0, op0=ALU.mult, op1=ALU.add
             )
 
         build_trig(0)
@@ -185,12 +190,12 @@ def tile_attention_pa_t_kernel(tc, x, pos0, pos1, wq, wk, out_0, out_1):
             codes, scales = quantised[step]
             products[step] = []
             for bank in range(STEP_BANKS):
-                product = prod_psum.tile([P, BANK_TILES, 2 * HEADS, PAIRS, 2], F32, name="product")
+                product = prod_psum.tile([P, BANK_TILES, PAIRS, 2, SETS], F32, name="product")
                 for j in range(BANK_TILES):
                     i = bank * BANK_TILES + j
                     for g in range(PASSES):
                         nc.tensor.matmul_mx(
-                            out=product[:, j].rearrange("p c r e -> p (c r e)"),
+                            out=product[:, j].rearrange("p r e c -> p (r e c)"),
                             lhsT=codes[:, i, g, :].bitcast(FP8X4),
                             lhsT_scale=scales[:, i, g, :],
                             rhs=w_codes[:, g, :].bitcast(FP8X4),
@@ -201,30 +206,36 @@ def tile_attention_pa_t_kernel(tc, x, pos0, pos1, wq, wk, out_0, out_1):
                 products[step].append(product)
 
         def rotate_and_store(step):
-            spread = [P, 2 * HEADS, PAIRS, 2]
-            from_re = work.tile([P, STEP_TILES] + spread[1:], F32, name="from_re")
-            from_im = work.tile([P, STEP_TILES] + spread[1:], F32, name="from_im")
-            for i in range(STEP_TILES):
-                product = products[step][i // BANK_TILES][:, i % BANK_TILES]
-                t = step * STEP_TILES + i
-                for part, result, low_row in ((0, from_re, 1), (1, from_im, 0)):
+            from_re = work.tile([P, SETS, STEP_TILES, PAIRS, 2], F32, name="from_re")
+            from_im = work.tile([P, SETS, STEP_TILES, PAIRS, 2], F32, name="from_im")
+            spread = [P, SETS, BANK_TILES * PAIRS, 2]
+            for bank in range(STEP_BANKS):
+                first = bank * BANK_TILES
+                t = step * STEP_TILES + first
+                for part, result, low_table in ((0, from_re, 1), (1, from_im, 0)):
                     nc.vector.tensor_tensor(
-                        out=result[:, i],
-                        in0=product[:, :, :, part : part + 1].to_broadcast(spread),
-                        in1=trig[:, t, low_row : low_row + 2, :].rearrange("p e r -> p r e").unsqueeze(1).to_broadcast(spread),
+                        out=result[:, :, first : first + BANK_TILES].rearrange("p c t r e -> p c (t r) e"),
+                        in0=products[step][bank][:, :, :, part, :]
+                        .rearrange("p t r c -> p c (t r)")
+                        .unsqueeze(3)
+                        .to_broadcast(spread),
+                        in1=trig[:, low_table : low_table + 2, t : t + BANK_TILES, :]
+                        .rearrange("p e t r -> p (t r) e")
+                        .unsqueeze(1)
+                        .to_broadcast(spread),
                         op=ALU.mult,
                     )
-            rotated = work.tile([P, 2, STEP_TILES, FEATURES], F32, name="rotated")
+            rotated = work.tile([P, STEP_TILES, SETS, 2 * PAIRS], F32, name="rotated")
             nc.gpsimd.tensor_tensor(
-                out=rotated[:].rearrange("p w t f -> p t w f"),
-                in0=from_re[:].rearrange("p t (w h) r e -> p t w (h r e)", w=2),
-                in1=from_im[:].rearrange("p t (w h) r e -> p t w (h r e)", w=2),
+                out=rotated[:],
+                in0=from_re[:].rearrange("p c t r e -> p t c (r e)"),
+                in1=from_im[:].rearrange("p c t r e -> p t c (r e)"),
                 op=ALU.add,
             )
             for which in range(2):
                 nc.sync.dma_start(
                     out=out_views[which][:, step * STEP_TILES : (step + 1) * STEP_TILES, :],
-                    in_=rotated[:, which],
+                    in_=rotated[:, :, which * HEADS : (which + 1) * HEADS, :].rearrange("p t h f -> p t (h f)"),
                 )
 
         for step in range(STEPS + 2):

@@ -17,7 +17,6 @@ TOKENS = 256
 DIM = 1024
 HEADS, PAIRS = 2, 32
 FEATURES = HEADS * PAIRS * 2
-SETS = 2 * HEADS
 FREQS = PAIRS // 2
 BASE = 10000.0
 
@@ -33,6 +32,7 @@ STEP_BANKS = STEP_TILES // BANK_TILES
 LOADS_AHEAD = 7
 TRIG_STEPS = 4
 TRIG_TILES = TRIG_STEPS * STEP_TILES
+TRIG_PARTS = TILES // TRIG_TILES
 
 FLOPS = 2 * BATCH * TOKENS * DIM * 2 * FEATURES
 
@@ -45,8 +45,8 @@ def transpose_rows(nc, psum, rows, identity):
     return flipped
 
 
-def group_pairs(nc, grouped, flipped):
-    nc.scalar.copy(
+def group_pairs(copy, grouped, flipped):
+    copy(
         out=grouped.bitcast(F32),
         in_=flipped[:].rearrange("p (g u) r -> p g r u", u=2),
     )
@@ -58,18 +58,19 @@ def tile_attention_pa_t_kernel(tc, x, pos0, pos1, wq, wk, out_0, out_1):
     out_views = [o.rearrange("b (r t) h f -> (b r) t (h f)", t=TILES) for o in (out_0, out_1)]
 
     with ExitStack() as ctx:
+        ctx.enter_context(tc.manual_schedule())
         const = ctx.enter_context(tc.tile_pool(name="const", bufs=1))
         x_pool = ctx.enter_context(tc.tile_pool(name="x_rows", bufs=LOADS_AHEAD + 1))
         work = ctx.enter_context(tc.tile_pool(name="work", bufs=3))
         flip_psum = ctx.enter_context(tc.psum_pool(name="flip_psum", bufs=4))
 
+        pos0_rows = const.tile([BATCH, ROWS], BF16)
+        pos1_rows = const.tile([BATCH, COLS], BF16)
+        nc.scalar.dma_start(out=pos0_rows[:], in_=pos0)
+        nc.scalar.dma_start(out=pos1_rows[:], in_=pos1)
         w_rows = const.tile([P, 2, DIM], BF16)
-        for which, w in enumerate((wq, wk)):
-            for h in range(HEADS):
-                nc.sync.dma_start(
-                    out=w_rows[which * HEADS + h : P : SETS, :, :],
-                    in_=w[h * 2 * PAIRS : (h + 1) * 2 * PAIRS, :].rearrange("(a j) k -> j a k", a=2),
-                )
+        nc.sync.dma_start(out=w_rows[:, 0, :], in_=wq)
+        nc.sync.dma_start(out=w_rows[:, 1, :], in_=wk)
 
         x_rows = {}
 
@@ -81,47 +82,32 @@ def tile_attention_pa_t_kernel(tc, x, pos0, pos1, wq, wk, out_0, out_1):
         for step in range(LOADS_AHEAD):
             load(step)
 
-        pos0_rows = const.tile([P, ROWS], BF16)
-        pos1_rows = const.tile([P, COLS], BF16)
-        nc.vector.memset(pos0_rows[:], 0.0)
-        nc.vector.memset(pos1_rows[:], 0.0)
-        nc.scalar.dma_start(out=pos0_rows[0:BATCH, :], in_=pos0)
-        nc.scalar.dma_start(out=pos1_rows[0:BATCH, :], in_=pos1)
-
         ones = const.tile([P, 1], F32)
         nc.vector.memset(ones[:], 1.0)
         first_sin = const.tile([P, 1], F32)
         nc.scalar.activation(out=first_sin[:], in_=ones[:], func=ACT.Sin)
-
         identity = const.tile([P, P], F32)
         make_identity(nc, identity[:])
-
-        w_grouped = const.tile([P, PASSES, 2, P, PACK], BF16, align_bytes=64)
-        for half in range(2):
-            flipped = transpose_rows(nc, flip_psum, w_rows[:, half, :], identity[:])
-            group_pairs(nc, w_grouped[:, :, half, :, :], flipped)
-        w_codes = const.tile([P, PASSES, 2 * P], U32, align_bytes=64)
-        w_scales = const.tile([P, PASSES, 2 * P], U8, align_bytes=64)
-        nc.vector.quantize_mx(
-            out=w_codes[:].rearrange("p g n -> p (g n)").bitcast(FP8X4),
-            scales=w_scales[:].rearrange("p g n -> p (g n)"),
-            in_=w_grouped[:].rearrange("p g w n j -> p (g w n j)"),
-        )
-
-        coords = const.tile([P, 2, TOKENS], BF16)
-        nc.vector.memset(coords[:, :, 0:1], 0.0)
-        nc.vector.tensor_copy(
-            out=coords[:, 0, 1:TOKENS].rearrange("b (i j) -> b i j", j=COLS),
-            in_=pos0_rows[:].unsqueeze(2).to_broadcast([P, ROWS, COLS]),
-        )
-        nc.vector.tensor_copy(
-            out=coords[:, 1, 1:TOKENS].rearrange("b (i j) -> b i j", j=COLS),
-            in_=pos1_rows[:].unsqueeze(1).to_broadcast([P, ROWS, COLS]),
-        )
+        theta = const.tile([P, FREQS], F32)
+        for m in range(FREQS):
+            nc.vector.tensor_scalar(
+                out=theta[:, m : m + 1], in0=ones[:], scalar1=1.0 / BASE ** (m / FREQS), scalar2=None, op0=ALU.mult
+            )
         send = const.tile([P, QUARTERS, BATCH, QUARTERS], BF16)
         nc.vector.memset(send[:], 0.0)
         for r in range(QUARTERS):
             nc.vector.tensor_copy(out=send[:, r, :, r], in_=identity[:, 0:BATCH])
+
+        coords = const.tile([P, 2, TOKENS], BF16)
+        nc.vector.memset(coords[:], 0.0)
+        nc.vector.tensor_copy(
+            out=coords[0:BATCH, 0, 1:TOKENS].rearrange("b (i j) -> b i j", j=COLS),
+            in_=pos0_rows[:].unsqueeze(2).to_broadcast([BATCH, ROWS, COLS]),
+        )
+        nc.vector.tensor_copy(
+            out=coords[0:BATCH, 1, 1:TOKENS].rearrange("b (i j) -> b i j", j=COLS),
+            in_=pos1_rows[:].unsqueeze(1).to_broadcast([BATCH, ROWS, COLS]),
+        )
         own_coords = const.tile([P, 2, TILES], F32)
         with tc.psum_pool(name="coord_psum", bufs=1) as coord_psum:
             sent = coord_psum.tile([P, 2, TILES], F32)
@@ -136,34 +122,61 @@ def tile_attention_pa_t_kernel(tc, x, pos0, pos1, wq, wk, out_0, out_1):
                     )
             nc.vector.tensor_copy(out=own_coords[:], in_=sent[:])
         prod_psum = ctx.enter_context(tc.psum_pool(name="prod_psum", bufs=2 * STEP_BANKS))
-        theta = const.tile([P, FREQS], F32)
-        for m in range(FREQS):
-            nc.vector.tensor_scalar(
-                out=theta[:, m : m + 1], in0=ones[:], scalar1=1.0 / BASE ** (m / FREQS), scalar2=None, op0=ALU.mult
-            )
-        angle = const.tile([P, TILES, 2, FREQS], F32)
-        nc.vector.tensor_tensor(
-            out=angle[:],
-            in0=own_coords[:].rearrange("p a t -> p t a").unsqueeze(3).to_broadcast([P, TILES, 2, FREQS]),
-            in1=theta[:].unsqueeze(1).unsqueeze(2).to_broadcast([P, TILES, 2, FREQS]),
-            op=ALU.mult,
-        )
-        trig = const.tile([P, 3, TILES, PAIRS], F32)
 
-        def build_trig(part):
-            tiles = slice(part * TRIG_TILES, (part + 1) * TRIG_TILES)
+        angle = const.tile([P, TILES, 2, FREQS], F32)
+        trig = const.tile([P, TILES, 3, PAIRS], F32)
+        half_sin_squares = {}
+
+        def part_tiles(part):
+            return slice(part * TRIG_TILES, (part + 1) * TRIG_TILES)
+
+        def angles(part):
+            spread = [P, TRIG_TILES, 2, FREQS]
+            nc.vector.tensor_tensor(
+                out=angle[:, part_tiles(part)],
+                in0=own_coords[:, :, part_tiles(part)].rearrange("p a t -> p t a").unsqueeze(3).to_broadcast(spread),
+                in1=theta[:].unsqueeze(1).unsqueeze(2).to_broadcast(spread),
+                op=ALU.mult,
+            )
+
+        def sines(part):
+            tiles = part_tiles(part)
             angle_pairs = angle[:, tiles].rearrange("p t a m -> p t (a m)")
             half_sin = work.tile([P, TRIG_TILES, PAIRS], F32, name="half_sin")
             half_sin_sq = work.tile([P, TRIG_TILES, PAIRS], F32, name="half_sin_sq")
             nc.scalar.activation(out=half_sin[:], in_=angle_pairs, func=ACT.Sin, scale=0.5)
             nc.scalar.activation(out=half_sin_sq[:], in_=half_sin[:], func=ACT.Square)
-            nc.scalar.activation(out=trig[:, 2, tiles, :], in_=angle_pairs, func=ACT.Sin)
-            nc.scalar.activation(out=trig[:, 0, tiles, :], in_=angle_pairs, func=ACT.Sin, scale=-1.0)
+            nc.scalar.activation(out=trig[:, tiles, 2, :], in_=angle_pairs, func=ACT.Sin)
+            nc.scalar.activation(out=trig[:, tiles, 0, :], in_=angle_pairs, func=ACT.Sin, scale=-1.0)
+            half_sin_squares[part] = half_sin_sq
+
+        def cosines(part):
             nc.vector.tensor_scalar(
-                out=trig[:, 1, tiles, :], in0=half_sin_sq[:], scalar1=-2.0, scalar2=1.0, op0=ALU.mult, op1=ALU.add
+                out=trig[:, part_tiles(part), 1, :],
+                in0=half_sin_squares[part][:],
+                scalar1=-2.0,
+                scalar2=1.0,
+                op0=ALU.mult,
+                op1=ALU.add,
             )
 
-        build_trig(0)
+        angles(0)
+        sines(0)
+
+        w_grouped = const.tile([P, PASSES, 2, P, PACK], BF16, align_bytes=64)
+        for which in range(2):
+            flipped = transpose_rows(nc, flip_psum, w_rows[:, which, :], identity[:])
+            group_pairs(nc.vector.tensor_copy, w_grouped[:, :, which, :, :], flipped)
+        w_codes = const.tile([P, PASSES, 2 * P], U32, align_bytes=64)
+        w_scales = const.tile([P, PASSES, 2 * P], U8, align_bytes=64)
+        nc.vector.quantize_mx(
+            out=w_codes[:].rearrange("p g n -> p (g n)").bitcast(FP8X4),
+            scales=w_scales[:].rearrange("p g n -> p (g n)"),
+            in_=w_grouped[:].rearrange("p g w n j -> p (g w n j)"),
+        )
+        for part in range(1, TRIG_PARTS):
+            angles(part)
+        cosines(0)
 
         grouped_rows = {}
         quantised = {}
@@ -173,7 +186,7 @@ def tile_attention_pa_t_kernel(tc, x, pos0, pos1, wq, wk, out_0, out_1):
             grouped = work.tile([P, STEP_TILES, PASSES, P, PACK], BF16, align_bytes=64, name="grouped")
             for i in range(STEP_TILES):
                 flipped = transpose_rows(nc, flip_psum, x_rows[step][:, i, :], identity[:])
-                group_pairs(nc, grouped[:, i], flipped)
+                group_pairs(nc.scalar.copy, grouped[:, i], flipped)
             grouped_rows[step] = grouped
 
         def quantise(step):
@@ -190,12 +203,12 @@ def tile_attention_pa_t_kernel(tc, x, pos0, pos1, wq, wk, out_0, out_1):
             codes, scales = quantised[step]
             products[step] = []
             for bank in range(STEP_BANKS):
-                product = prod_psum.tile([P, BANK_TILES, PAIRS, 2, SETS], F32, name="product")
+                product = prod_psum.tile([P, BANK_TILES, 2 * HEADS, PAIRS, 2], F32, name="product")
                 for j in range(BANK_TILES):
                     i = bank * BANK_TILES + j
                     for g in range(PASSES):
                         nc.tensor.matmul_mx(
-                            out=product[:, j].rearrange("p r e c -> p (r e c)"),
+                            out=product[:, j].rearrange("p c r e -> p (c r e)"),
                             lhsT=codes[:, i, g, :].bitcast(FP8X4),
                             lhsT_scale=scales[:, i, g, :],
                             rhs=w_codes[:, g, :].bitcast(FP8X4),
@@ -206,48 +219,46 @@ def tile_attention_pa_t_kernel(tc, x, pos0, pos1, wq, wk, out_0, out_1):
                 products[step].append(product)
 
         def rotate_and_store(step):
-            from_re = work.tile([P, SETS, STEP_TILES, PAIRS, 2], F32, name="from_re")
-            from_im = work.tile([P, SETS, STEP_TILES, PAIRS, 2], F32, name="from_im")
-            spread = [P, SETS, BANK_TILES * PAIRS, 2]
-            for bank in range(STEP_BANKS):
-                first = bank * BANK_TILES
-                t = step * STEP_TILES + first
-                for part, result, low_table in ((0, from_re, 1), (1, from_im, 0)):
+            spread = [P, 2 * HEADS, PAIRS, 2]
+            from_re = work.tile([P, STEP_TILES] + spread[1:], F32, name="from_re")
+            from_im = work.tile([P, STEP_TILES] + spread[1:], F32, name="from_im")
+            for i in range(STEP_TILES):
+                product = products[step][i // BANK_TILES][:, i % BANK_TILES]
+                t = step * STEP_TILES + i
+                for part, result, low_row in ((0, from_re, 1), (1, from_im, 0)):
                     nc.vector.tensor_tensor(
-                        out=result[:, :, first : first + BANK_TILES].rearrange("p c t r e -> p c (t r) e"),
-                        in0=products[step][bank][:, :, :, part, :]
-                        .rearrange("p t r c -> p c (t r)")
-                        .unsqueeze(3)
-                        .to_broadcast(spread),
-                        in1=trig[:, low_table : low_table + 2, t : t + BANK_TILES, :]
-                        .rearrange("p e t r -> p (t r) e")
-                        .unsqueeze(1)
-                        .to_broadcast(spread),
+                        out=result[:, i],
+                        in0=product[:, :, :, part : part + 1].to_broadcast(spread),
+                        in1=trig[:, t, low_row : low_row + 2, :].rearrange("p e r -> p r e").unsqueeze(1).to_broadcast(spread),
                         op=ALU.mult,
                     )
-            rotated = work.tile([P, STEP_TILES, SETS, 2 * PAIRS], F32, name="rotated")
+            rotated = work.tile([P, 2, STEP_TILES, FEATURES], F32, name="rotated")
             nc.gpsimd.tensor_tensor(
-                out=rotated[:],
-                in0=from_re[:].rearrange("p c t r e -> p t c (r e)"),
-                in1=from_im[:].rearrange("p c t r e -> p t c (r e)"),
+                out=rotated[:].rearrange("p w t f -> p t w f"),
+                in0=from_re[:].rearrange("p t (w h) r e -> p t w (h r e)", w=2),
+                in1=from_im[:].rearrange("p t (w h) r e -> p t w (h r e)", w=2),
                 op=ALU.add,
             )
             for which in range(2):
                 nc.sync.dma_start(
                     out=out_views[which][:, step * STEP_TILES : (step + 1) * STEP_TILES, :],
-                    in_=rotated[:, :, which * HEADS : (which + 1) * HEADS, :].rearrange("p t h f -> p t (h f)"),
+                    in_=rotated[:, which],
                 )
 
         for step in range(STEPS + 2):
+            next_part = step // TRIG_STEPS + 1
+            build_next_part = step % TRIG_STEPS == 0 and next_part < TRIG_PARTS
             if step + LOADS_AHEAD < STEPS:
                 load(step + LOADS_AHEAD)
             if step < STEPS:
                 transpose_and_group(step)
+            if build_next_part:
+                sines(next_part)
             if 1 <= step <= STEPS:
                 project(step - 1)
             if step >= 2:
                 rotate_and_store(step - 2)
             if step < STEPS:
                 quantise(step)
-            if step % TRIG_STEPS == 0 and step + TRIG_STEPS < STEPS:
-                build_trig(step // TRIG_STEPS + 1)
+            if build_next_part:
+                cosines(next_part)

@@ -17,6 +17,7 @@ TOKENS = 256
 DIM = 1024
 HEADS, PAIRS = 2, 32
 FEATURES = HEADS * PAIRS * 2
+SETS = 2 * HEADS
 FREQS = PAIRS // 2
 BASE = 10000.0
 
@@ -69,8 +70,12 @@ def tile_attention_pa_t_kernel(tc, x, pos0, pos1, wq, wk, out_0, out_1):
         nc.scalar.dma_start(out=pos0_rows[:], in_=pos0)
         nc.scalar.dma_start(out=pos1_rows[:], in_=pos1)
         w_rows = const.tile([P, 2, DIM], BF16)
-        nc.sync.dma_start(out=w_rows[:, 0, :], in_=wq)
-        nc.sync.dma_start(out=w_rows[:, 1, :], in_=wk)
+        for which, weights in enumerate((wq, wk)):
+            for h in range(HEADS):
+                nc.sync.dma_start(
+                    out=w_rows[which * HEADS + h : P : SETS, :, :],
+                    in_=weights[h * 2 * PAIRS : (h + 1) * 2 * PAIRS, :].rearrange("(a j) k -> j a k", a=2),
+                )
 
         x_rows = {}
 
@@ -124,7 +129,7 @@ def tile_attention_pa_t_kernel(tc, x, pos0, pos1, wq, wk, out_0, out_1):
         prod_psum = ctx.enter_context(tc.psum_pool(name="prod_psum", bufs=2 * STEP_BANKS))
 
         angle = const.tile([P, TILES, 2, FREQS], F32)
-        trig = const.tile([P, TILES, 3, PAIRS], F32)
+        trig = const.tile([P, 3, TILES, PAIRS], F32)
         half_sin_squares = {}
 
         def part_tiles(part):
@@ -146,13 +151,13 @@ def tile_attention_pa_t_kernel(tc, x, pos0, pos1, wq, wk, out_0, out_1):
             half_sin_sq = work.tile([P, TRIG_TILES, PAIRS], F32, name="half_sin_sq")
             nc.scalar.activation(out=half_sin[:], in_=angle_pairs, func=ACT.Sin, scale=0.5)
             nc.scalar.activation(out=half_sin_sq[:], in_=half_sin[:], func=ACT.Square)
-            nc.scalar.activation(out=trig[:, tiles, 2, :], in_=angle_pairs, func=ACT.Sin)
-            nc.scalar.activation(out=trig[:, tiles, 0, :], in_=angle_pairs, func=ACT.Sin, scale=-1.0)
+            nc.scalar.activation(out=trig[:, 2, tiles, :], in_=angle_pairs, func=ACT.Sin)
+            nc.scalar.activation(out=trig[:, 0, tiles, :], in_=angle_pairs, func=ACT.Sin, scale=-1.0)
             half_sin_squares[part] = half_sin_sq
 
         def cosines(part):
             nc.vector.tensor_scalar(
-                out=trig[:, part_tiles(part), 1, :],
+                out=trig[:, 1, part_tiles(part), :],
                 in0=half_sin_squares[part][:],
                 scalar1=-2.0,
                 scalar2=1.0,
@@ -164,9 +169,9 @@ def tile_attention_pa_t_kernel(tc, x, pos0, pos1, wq, wk, out_0, out_1):
         sines(0)
 
         w_grouped = const.tile([P, PASSES, 2, P, PACK], BF16, align_bytes=64)
-        for which in range(2):
-            flipped = transpose_rows(nc, flip_psum, w_rows[:, which, :], identity[:])
-            group_pairs(nc.vector.tensor_copy, w_grouped[:, :, which, :, :], flipped)
+        for half in range(2):
+            flipped = transpose_rows(nc, flip_psum, w_rows[:, half, :], identity[:])
+            group_pairs(nc.vector.tensor_copy, w_grouped[:, :, half, :, :], flipped)
         w_codes = const.tile([P, PASSES, 2 * P], U32, align_bytes=64)
         w_scales = const.tile([P, PASSES, 2 * P], U8, align_bytes=64)
         nc.vector.quantize_mx(
@@ -203,12 +208,12 @@ def tile_attention_pa_t_kernel(tc, x, pos0, pos1, wq, wk, out_0, out_1):
             codes, scales = quantised[step]
             products[step] = []
             for bank in range(STEP_BANKS):
-                product = prod_psum.tile([P, BANK_TILES, 2 * HEADS, PAIRS, 2], F32, name="product")
+                product = prod_psum.tile([P, BANK_TILES, PAIRS, 2, SETS], F32, name="product")
                 for j in range(BANK_TILES):
                     i = bank * BANK_TILES + j
                     for g in range(PASSES):
                         nc.tensor.matmul_mx(
-                            out=product[:, j].rearrange("p c r e -> p (c r e)"),
+                            out=product[:, j].rearrange("p r e c -> p (r e c)"),
                             lhsT=codes[:, i, g, :].bitcast(FP8X4),
                             lhsT_scale=scales[:, i, g, :],
                             rhs=w_codes[:, g, :].bitcast(FP8X4),
@@ -219,30 +224,37 @@ def tile_attention_pa_t_kernel(tc, x, pos0, pos1, wq, wk, out_0, out_1):
                 products[step].append(product)
 
         def rotate_and_store(step):
-            spread = [P, 2 * HEADS, PAIRS, 2]
-            from_re = work.tile([P, STEP_TILES] + spread[1:], F32, name="from_re")
-            from_im = work.tile([P, STEP_TILES] + spread[1:], F32, name="from_im")
-            for i in range(STEP_TILES):
-                product = products[step][i // BANK_TILES][:, i % BANK_TILES]
-                t = step * STEP_TILES + i
-                for part, result, low_row in ((0, from_re, 1), (1, from_im, 0)):
+            from_re = work.tile([P, SETS, STEP_TILES, PAIRS, 2], F32, name="from_re")
+            from_im = work.tile([P, SETS, STEP_TILES, PAIRS, 2], F32, name="from_im")
+            spread = [P, SETS, BANK_TILES * PAIRS, 2]
+            for bank in range(STEP_BANKS):
+                first = bank * BANK_TILES
+                t = step * STEP_TILES + first
+                for part, result, low_table in ((0, from_re, 1), (1, from_im, 0)):
                     nc.vector.tensor_tensor(
-                        out=result[:, i],
-                        in0=product[:, :, :, part : part + 1].to_broadcast(spread),
-                        in1=trig[:, t, low_row : low_row + 2, :].rearrange("p e r -> p r e").unsqueeze(1).to_broadcast(spread),
+                        out=result[:, :, first : first + BANK_TILES].rearrange("p c t r e -> p c (t r) e"),
+                        in0=products[step][bank][:, :, :, part, :]
+                        .rearrange("p t r c -> p c (t r)")
+                        .unsqueeze(3)
+                        .to_broadcast(spread),
+                        in1=trig[:, low_table : low_table + 2, t : t + BANK_TILES, :]
+                        .rearrange("p e t r -> p (t r) e")
+                        .unsqueeze(1)
+                        .to_broadcast(spread),
                         op=ALU.mult,
                     )
-            rotated = work.tile([P, 2, STEP_TILES, FEATURES], F32, name="rotated")
-            nc.gpsimd.tensor_tensor(
-                out=rotated[:].rearrange("p w t f -> p t w f"),
-                in0=from_re[:].rearrange("p t (w h) r e -> p t w (h r e)", w=2),
-                in1=from_im[:].rearrange("p t (w h) r e -> p t w (h r e)", w=2),
-                op=ALU.add,
-            )
+            rotated = work.tile([P, 2, STEP_TILES, HEADS, 2 * PAIRS], F32, name="rotated")
             for which in range(2):
+                sets = slice(which * HEADS, (which + 1) * HEADS)
+                nc.gpsimd.tensor_tensor(
+                    out=rotated[:, which],
+                    in0=from_re[:, sets].rearrange("p h t r e -> p t h (r e)"),
+                    in1=from_im[:, sets].rearrange("p h t r e -> p t h (r e)"),
+                    op=ALU.add,
+                )
                 nc.sync.dma_start(
                     out=out_views[which][:, step * STEP_TILES : (step + 1) * STEP_TILES, :],
-                    in_=rotated[:, which],
+                    in_=rotated[:, which].rearrange("p t h f -> p t (h f)"),
                 )
 
         for step in range(STEPS + 2):

@@ -17,7 +17,6 @@ TOKENS = 256
 DIM = 1024
 HEADS, PAIRS = 2, 32
 FEATURES = HEADS * PAIRS * 2
-SETS = 2 * HEADS
 FREQS = PAIRS // 2
 BASE = 10000.0
 
@@ -67,15 +66,11 @@ def tile_attention_pa_t_kernel(tc, x, pos0, pos1, wq, wk, out_0, out_1):
 
         pos0_rows = const.tile([BATCH, ROWS], BF16)
         pos1_rows = const.tile([BATCH, COLS], BF16)
-        nc.scalar.dma_start(out=pos0_rows[:], in_=pos0)
-        nc.scalar.dma_start(out=pos1_rows[:], in_=pos1)
+        nc.sync.dma_start(out=pos0_rows[:], in_=pos0)
+        nc.sync.dma_start(out=pos1_rows[:], in_=pos1)
         w_rows = const.tile([P, 2, DIM], BF16)
-        for which, weights in enumerate((wq, wk)):
-            for h in range(HEADS):
-                nc.sync.dma_start(
-                    out=w_rows[which * HEADS + h : P : SETS, :, :],
-                    in_=weights[h * 2 * PAIRS : (h + 1) * 2 * PAIRS, :].rearrange("(a j) k -> j a k", a=2),
-                )
+        nc.sync.dma_start(out=w_rows[:, 0, :], in_=wq)
+        nc.sync.dma_start(out=w_rows[:, 1, :], in_=wk)
 
         x_rows = {}
 
@@ -93,11 +88,6 @@ def tile_attention_pa_t_kernel(tc, x, pos0, pos1, wq, wk, out_0, out_1):
         nc.scalar.activation(out=first_sin[:], in_=ones[:], func=ACT.Sin)
         identity = const.tile([P, P], F32)
         make_identity(nc, identity[:])
-        theta = const.tile([P, FREQS], F32)
-        for m in range(FREQS):
-            nc.vector.tensor_scalar(
-                out=theta[:, m : m + 1], in0=ones[:], scalar1=1.0 / BASE ** (m / FREQS), scalar2=None, op0=ALU.mult
-            )
         send = const.tile([P, QUARTERS, BATCH, QUARTERS], BF16)
         nc.vector.memset(send[:], 0.0)
         for r in range(QUARTERS):
@@ -113,6 +103,11 @@ def tile_attention_pa_t_kernel(tc, x, pos0, pos1, wq, wk, out_0, out_1):
             out=coords[0:BATCH, 1, 1:TOKENS].rearrange("b (i j) -> b i j", j=COLS),
             in_=pos1_rows[:].unsqueeze(1).to_broadcast([BATCH, ROWS, COLS]),
         )
+        theta = const.tile([P, FREQS], F32)
+        for m in range(FREQS):
+            nc.vector.tensor_scalar(
+                out=theta[:, m : m + 1], in0=ones[:], scalar1=1.0 / BASE ** (m / FREQS), scalar2=None, op0=ALU.mult
+            )
         own_coords = const.tile([P, 2, TILES], F32)
         with tc.psum_pool(name="coord_psum", bufs=1) as coord_psum:
             sent = coord_psum.tile([P, 2, TILES], F32)
@@ -129,7 +124,7 @@ def tile_attention_pa_t_kernel(tc, x, pos0, pos1, wq, wk, out_0, out_1):
         prod_psum = ctx.enter_context(tc.psum_pool(name="prod_psum", bufs=2 * STEP_BANKS))
 
         angle = const.tile([P, TILES, 2, FREQS], F32)
-        trig = const.tile([P, 3, TILES, PAIRS], F32)
+        trig = const.tile([P, TILES, 3, PAIRS], F32)
         half_sin_squares = {}
 
         def part_tiles(part):
@@ -151,13 +146,13 @@ def tile_attention_pa_t_kernel(tc, x, pos0, pos1, wq, wk, out_0, out_1):
             half_sin_sq = work.tile([P, TRIG_TILES, PAIRS], F32, name="half_sin_sq")
             nc.scalar.activation(out=half_sin[:], in_=angle_pairs, func=ACT.Sin, scale=0.5)
             nc.scalar.activation(out=half_sin_sq[:], in_=half_sin[:], func=ACT.Square)
-            nc.scalar.activation(out=trig[:, 2, tiles, :], in_=angle_pairs, func=ACT.Sin)
-            nc.scalar.activation(out=trig[:, 0, tiles, :], in_=angle_pairs, func=ACT.Sin, scale=-1.0)
+            nc.scalar.activation(out=trig[:, tiles, 2, :], in_=angle_pairs, func=ACT.Sin)
+            nc.scalar.activation(out=trig[:, tiles, 0, :], in_=angle_pairs, func=ACT.Sin, scale=-1.0)
             half_sin_squares[part] = half_sin_sq
 
         def cosines(part):
             nc.vector.tensor_scalar(
-                out=trig[:, 1, part_tiles(part), :],
+                out=trig[:, part_tiles(part), 1, :],
                 in0=half_sin_squares[part][:],
                 scalar1=-2.0,
                 scalar2=1.0,
@@ -169,9 +164,9 @@ def tile_attention_pa_t_kernel(tc, x, pos0, pos1, wq, wk, out_0, out_1):
         sines(0)
 
         w_grouped = const.tile([P, PASSES, 2, P, PACK], BF16, align_bytes=64)
-        for half in range(2):
-            flipped = transpose_rows(nc, flip_psum, w_rows[:, half, :], identity[:])
-            group_pairs(nc.vector.tensor_copy, w_grouped[:, :, half, :, :], flipped)
+        for which in range(2):
+            flipped = transpose_rows(nc, flip_psum, w_rows[:, which, :], identity[:])
+            group_pairs(nc.vector.tensor_copy, w_grouped[:, :, which, :, :], flipped)
         w_codes = const.tile([P, PASSES, 2 * P], U32, align_bytes=64)
         w_scales = const.tile([P, PASSES, 2 * P], U8, align_bytes=64)
         nc.vector.quantize_mx(
@@ -208,12 +203,12 @@ def tile_attention_pa_t_kernel(tc, x, pos0, pos1, wq, wk, out_0, out_1):
             codes, scales = quantised[step]
             products[step] = []
             for bank in range(STEP_BANKS):
-                product = prod_psum.tile([P, BANK_TILES, PAIRS, 2, SETS], F32, name="product")
+                product = prod_psum.tile([P, BANK_TILES, 2 * HEADS, PAIRS, 2], F32, name="product")
                 for j in range(BANK_TILES):
                     i = bank * BANK_TILES + j
                     for g in range(PASSES):
                         nc.tensor.matmul_mx(
-                            out=product[:, j].rearrange("p r e c -> p (r e c)"),
+                            out=product[:, j].rearrange("p c r e -> p (c r e)"),
                             lhsT=codes[:, i, g, :].bitcast(FP8X4),
                             lhsT_scale=scales[:, i, g, :],
                             rhs=w_codes[:, g, :].bitcast(FP8X4),
@@ -223,43 +218,42 @@ def tile_attention_pa_t_kernel(tc, x, pos0, pos1, wq, wk, out_0, out_1):
                         )
                 products[step].append(product)
 
-        def rotate_and_store(step):
-            from_re = work.tile([P, SETS, STEP_TILES, PAIRS, 2], F32, name="from_re")
-            from_im = work.tile([P, SETS, STEP_TILES, PAIRS, 2], F32, name="from_im")
-            spread = [P, SETS, BANK_TILES * PAIRS, 2]
-            for bank in range(STEP_BANKS):
-                first = bank * BANK_TILES
-                t = step * STEP_TILES + first
-                for part, result, low_table in ((0, from_re, 1), (1, from_im, 0)):
-                    nc.vector.tensor_tensor(
-                        out=result[:, :, first : first + BANK_TILES].rearrange("p c t r e -> p c (t r) e"),
-                        in0=products[step][bank][:, :, :, part, :]
-                        .rearrange("p t r c -> p c (t r)")
-                        .unsqueeze(3)
-                        .to_broadcast(spread),
-                        in1=trig[:, low_table : low_table + 2, t : t + BANK_TILES, :]
-                        .rearrange("p e t r -> p (t r) e")
-                        .unsqueeze(1)
-                        .to_broadcast(spread),
-                        op=ALU.mult,
-                    )
-            rotated = work.tile([P, 2, STEP_TILES, HEADS, 2 * PAIRS], F32, name="rotated")
-            for which in range(2):
-                sets = slice(which * HEADS, (which + 1) * HEADS)
+        def rotate_and_store(step, pieces):
+            spread = [P, 2 * HEADS, PAIRS, 2]
+            from_re = work.tile([P, STEP_TILES] + spread[1:], F32, name="from_re")
+            from_im = work.tile([P, STEP_TILES] + spread[1:], F32, name="from_im")
+            rotated = work.tile([P, 2, STEP_TILES, FEATURES], F32, name="rotated")
+            run = STEP_TILES // pieces
+            for first in range(0, STEP_TILES, run):
+                for i in range(first, first + run):
+                    product = products[step][i // BANK_TILES][:, i % BANK_TILES]
+                    t = step * STEP_TILES + i
+                    for part, result, low_row in ((0, from_re, 1), (1, from_im, 0)):
+                        nc.vector.tensor_tensor(
+                            out=result[:, i],
+                            in0=product[:, :, :, part : part + 1].to_broadcast(spread),
+                            in1=trig[:, t, low_row : low_row + 2, :]
+                            .rearrange("p e r -> p r e")
+                            .unsqueeze(1)
+                            .to_broadcast(spread),
+                            op=ALU.mult,
+                        )
+                tiles = slice(first, first + run)
                 nc.gpsimd.tensor_tensor(
-                    out=rotated[:, which],
-                    in0=from_re[:, sets].rearrange("p h t r e -> p t h (r e)"),
-                    in1=from_im[:, sets].rearrange("p h t r e -> p t h (r e)"),
+                    out=rotated[:, :, tiles].rearrange("p w t f -> p t w f"),
+                    in0=from_re[:, tiles].rearrange("p t (w h) r e -> p t w (h r e)", w=2),
+                    in1=from_im[:, tiles].rearrange("p t (w h) r e -> p t w (h r e)", w=2),
                     op=ALU.add,
                 )
-                nc.sync.dma_start(
-                    out=out_views[which][:, step * STEP_TILES : (step + 1) * STEP_TILES, :],
-                    in_=rotated[:, which].rearrange("p t h f -> p t (h f)"),
-                )
+                for which in range(2):
+                    nc.sync.dma_start(
+                        out=out_views[which][:, step * STEP_TILES + first : step * STEP_TILES + first + run, :],
+                        in_=rotated[:, which, tiles],
+                    )
 
         for step in range(STEPS + 2):
             next_part = step // TRIG_STEPS + 1
-            build_next_part = step % TRIG_STEPS == 0 and next_part < TRIG_PARTS
+            build_next_part = step % TRIG_STEPS == TRIG_STEPS - 1 and next_part < TRIG_PARTS
             if step + LOADS_AHEAD < STEPS:
                 load(step + LOADS_AHEAD)
             if step < STEPS:
@@ -269,7 +263,7 @@ def tile_attention_pa_t_kernel(tc, x, pos0, pos1, wq, wk, out_0, out_1):
             if 1 <= step <= STEPS:
                 project(step - 1)
             if step >= 2:
-                rotate_and_store(step - 2)
+                rotate_and_store(step - 2, pieces=STEP_BANKS if step - 2 == STEPS - 1 else 1)
             if step < STEPS:
                 quantise(step)
             if build_next_part:

from contextlib import ExitStack

import concourse.mybir as mybir
from concourse.masks import make_identity

F32 = mybir.dt.float32
BF16 = mybir.dt.bfloat16
U32 = mybir.dt.uint32
U8 = mybir.dt.uint8
FP8X4 = mybir.dt.float8_e4m3fn_x4
ALU = mybir.AluOpType
ACT = mybir.ActivationFunctionType

P = 128
BATCH, ROWS, COLS = 32, 15, 17
TOKENS = 256
DIM = 1024
HEADS, PAIRS = 2, 32
FEATURES = HEADS * PAIRS * 2
FREQS = PAIRS // 2
BASE = 10000.0

QUARTERS = P // BATCH
TILES = TOKENS // QUARTERS
PACK = 4
PASSES = DIM // (P * PACK)
WORD_TILES = DIM // (2 * P)
STEP_TILES = 4
STEPS = TILES // STEP_TILES
BANK_TILES = 2
STEP_BANKS = STEP_TILES // BANK_TILES
LOADS_AHEAD = 7
TRIG_STEPS = 4
TRIG_TILES = TRIG_STEPS * STEP_TILES
TRIG_PARTS = TILES // TRIG_TILES

FLOPS = 2 * BATCH * TOKENS * DIM * 2 * FEATURES


def transpose_rows(nc, psum, rows, identity):
    words = rows.bitcast(F32)
    flipped = psum.tile([P, WORD_TILES, P], F32)
    for w in range(WORD_TILES):
        nc.tensor.transpose(flipped[:, w, :], words[:, w * P : (w + 1) * P], identity)
    return flipped


def group_pairs(copy, grouped, flipped):
    copy(
        out=grouped.bitcast(F32),
        in_=flipped[:].rearrange("p (g u) r -> p g r u", u=2),
    )


def tile_attention_pa_t_kernel(tc, x, pos0, pos1, wq, wk, out_0, out_1):
    nc = tc.nc
    x_view = x.rearrange("b (r t) k -> (b r) t k", t=TILES)
    out_views = [o.rearrange("b (r t) h f -> (b r) t (h f)", t=TILES) for o in (out_0, out_1)]

    with ExitStack() as ctx:
        ctx.enter_context(tc.manual_schedule())
        const = ctx.enter_context(tc.tile_pool(name="const", bufs=1))
        x_pool = ctx.enter_context(tc.tile_pool(name="x_rows", bufs=LOADS_AHEAD + 1))
        work = ctx.enter_context(tc.tile_pool(name="work", bufs=3))
        flip_psum = ctx.enter_context(tc.psum_pool(name="flip_psum", bufs=4))

        pos0_rows = const.tile([BATCH, ROWS], BF16)
        pos1_rows = const.tile([BATCH, COLS], BF16)
        nc.sync.dma_start(out=pos0_rows[:], in_=pos0)
        nc.sync.dma_start(out=pos1_rows[:], in_=pos1)
        w_rows = const.tile([P, 2, DIM], BF16)
        nc.sync.dma_start(out=w_rows[:, 0, :], in_=wq)
        nc.sync.dma_start(out=w_rows[:, 1, :], in_=wk)

        x_rows = {}

        def load(step):
            rows = x_pool.tile([P, STEP_TILES, DIM], BF16, name="rows")
            nc.sync.dma_start(out=rows[:], in_=x_view[:, step * STEP_TILES : (step + 1) * STEP_TILES, :])
            x_rows[step] = rows

        for step in range(LOADS_AHEAD):
            load(step)

        ones = const.tile([P, 1], F32)
        nc.vector.memset(ones[:], 1.0)
        first_sin = const.tile([P, 1], F32)
        nc.scalar.activation(out=first_sin[:], in_=ones[:], func=ACT.Sin)
        identity = const.tile([P, P], F32)
        make_identity(nc, identity[:])
        send = const.tile([P, QUARTERS, BATCH, QUARTERS], BF16)
        nc.vector.memset(send[:], 0.0)
        for r in range(QUARTERS):
            nc.vector.tensor_copy(out=send[:, r, :, r], in_=identity[:, 0:BATCH])

        coords = const.tile([P, 2, TOKENS], BF16)
        nc.vector.memset(coords[:], 0.0)
        nc.vector.tensor_copy(
            out=coords[0:BATCH, 0, 1:TOKENS].rearrange("b (i j) -> b i j", j=COLS),
            in_=pos0_rows[:].unsqueeze(2).to_broadcast([BATCH, ROWS, COLS]),
        )
        nc.vector.tensor_copy(
            out=coords[0:BATCH, 1, 1:TOKENS].rearrange("b (i j) -> b i j", j=COLS),
            in_=pos1_rows[:].unsqueeze(1).to_broadcast([BATCH, ROWS, COLS]),
        )
        theta = const.tile([P, FREQS], F32)
        for m in range(FREQS):
            nc.vector.tensor_scalar(
                out=theta[:, m : m + 1], in0=ones[:], scalar1=1.0 / BASE ** (m / FREQS), scalar2=None, op0=ALU.mult
            )
        own_coords = const.tile([P, 2, TILES], F32)
        with tc.psum_pool(name="coord_psum", bufs=1) as coord_psum:
            sent = coord_psum.tile([P, 2, TILES], F32)
            for axis in range(2):
                for r in range(QUARTERS):
                    nc.tensor.matmul(
                        out=sent[:, axis, :],
                        lhsT=send[:, r, :, :].rearrange("k b q -> k (b q)"),
                        rhs=coords[:, axis, r * TILES : (r + 1) * TILES],
                        start=(r == 0),
                        stop=(r == QUARTERS - 1),
                    )
            nc.vector.tensor_copy(out=own_coords[:], in_=sent[:])
        prod_psum = ctx.enter_context(tc.psum_pool(name="prod_psum", bufs=2 * STEP_BANKS))

        angle = const.tile([P, TILES, 2, FREQS], F32)
        trig = const.tile([P, TILES, 3, PAIRS], F32)
        half_sin_squares = {}

        def part_tiles(part):
            return slice(part * TRIG_TILES, (part + 1) * TRIG_TILES)

        def angles(part):
            spread = [P, TRIG_TILES, 2, FREQS]
            nc.vector.tensor_tensor(
                out=angle[:, part_tiles(part)],
                in0=own_coords[:, :, part_tiles(part)].rearrange("p a t -> p t a").unsqueeze(3).to_broadcast(spread),
                in1=theta[:].unsqueeze(1).unsqueeze(2).to_broadcast(spread),
                op=ALU.mult,
            )

        def sines(part):
            tiles = part_tiles(part)
            angle_pairs = angle[:, tiles].rearrange("p t a m -> p t (a m)")
            half_sin = work.tile([P, TRIG_TILES, PAIRS], F32, name="half_sin")
            half_sin_sq = work.tile([P, TRIG_TILES, PAIRS], F32, name="half_sin_sq")
            nc.scalar.activation(out=half_sin[:], in_=angle_pairs, func=ACT.Sin, scale=0.5)
            nc.scalar.activation(out=half_sin_sq[:], in_=half_sin[:], func=ACT.Square)
            nc.scalar.activation(out=trig[:, tiles, 2, :], in_=angle_pairs, func=ACT.Sin)
            nc.scalar.activation(out=trig[:, tiles, 0, :], in_=angle_pairs, func=ACT.Sin, scale=-1.0)
            half_sin_squares[part] = half_sin_sq

        def cosines(part):
            nc.vector.tensor_scalar(
                out=trig[:, part_tiles(part), 1, :],
                in0=half_sin_squares[part][:],
                scalar1=-2.0,
                scalar2=1.0,
                op0=ALU.mult,
                op1=ALU.add,
            )

        angles(0)
        sines(0)

        w_grouped = const.tile([P, PASSES, 2, P, PACK], BF16, align_bytes=64)
        for which in range(2):
            flipped = transpose_rows(nc, flip_psum, w_rows[:, which, :], identity[:])
            group_pairs(nc.vector.tensor_copy, w_grouped[:, :, which, :, :], flipped)
        w_codes = const.tile([P, PASSES, 2 * P], U32, align_bytes=64)
        w_scales = const.tile([P, PASSES, 2 * P], U8, align_bytes=64)
        nc.vector.quantize_mx(
            out=w_codes[:].rearrange("p g n -> p (g n)").bitcast(FP8X4),
            scales=w_scales[:].rearrange("p g n -> p (g n)"),
            in_=w_grouped[:].rearrange("p g w n j -> p (g w n j)"),
        )
        for part in range(1, TRIG_PARTS):
            angles(part)
        cosines(0)

        grouped_rows = {}
        quantised = {}
        products = {}

        def transpose_and_group(step):
            grouped = work.tile([P, STEP_TILES, PASSES, P, PACK], BF16, align_bytes=64, name="grouped")
            for i in range(STEP_TILES):
                flipped = transpose_rows(nc, flip_psum, x_rows[step][:, i, :], identity[:])
                group_pairs(nc.scalar.copy, grouped[:, i], flipped)
            grouped_rows[step] = grouped

        def quantise(step):
            codes = work.tile([P, STEP_TILES, PASSES, P], U32, align_bytes=64, name="codes")
            scales = work.tile([P, STEP_TILES, PASSES, P], U8, align_bytes=64, name="scales")
            nc.vector.quantize_mx(
                out=codes[:].rearrange("p t g r -> p (t g r)").bitcast(FP8X4),
                scales=scales[:].rearrange("p t g r -> p (t g r)"),
                in_=grouped_rows[step][:].rearrange("p t g r j -> p (t g r j)"),
            )
            quantised[step] = (codes, scales)

        def project(step):
            codes, scales = quantised[step]
            products[step] = []
            for bank in range(STEP_BANKS):
                product = prod_psum.tile([P, BANK_TILES, 2 * HEADS, PAIRS, 2], F32, name="product")
                for j in range(BANK_TILES):
                    i = bank * BANK_TILES + j
                    for g in range(PASSES):
                        nc.tensor.matmul_mx(
                            out=product[:, j].rearrange("p c r e -> p (c r e)"),
                            lhsT=codes[:, i, g, :].bitcast(FP8X4),
                            lhsT_scale=scales[:, i, g, :],
                            rhs=w_codes[:, g, :].bitcast(FP8X4),
                            rhs_scale=w_scales[:, g, :],
                            start=(g == 0),
                            stop=(g == PASSES - 1),
                        )
                products[step].append(product)

        def rotate_and_store(step, pieces):
            spread = [P, 2 * HEADS, PAIRS, 2]
            from_re = work.tile([P, STEP_TILES] + spread[1:], F32, name="from_re")
            from_im = work.tile([P, STEP_TILES] + spread[1:], F32, name="from_im")
            rotated = work.tile([P, 2, STEP_TILES, FEATURES], F32, name="rotated")
            run = STEP_TILES // pieces
            for first in range(0, STEP_TILES, run):
                for i in range(first, first + run):
                    product = products[step][i // BANK_TILES][:, i % BANK_TILES]
                    t = step * STEP_TILES + i
                    for part, result, low_row in ((0, from_re, 1), (1, from_im, 0)):
                        nc.vector.tensor_tensor(
                            out=result[:, i],
                            in0=product[:, :, :, part : part + 1].to_broadcast(spread),
                            in1=trig[:, t, low_row : low_row + 2, :]
                            .rearrange("p e r -> p r e")
                            .unsqueeze(1)
                            .to_broadcast(spread),
                            op=ALU.mult,
                        )
                tiles = slice(first, first + run)
                nc.gpsimd.tensor_tensor(
                    out=rotated[:, :, tiles].rearrange("p w t f -> p t w f"),
                    in0=from_re[:, tiles].rearrange("p t (w h) r e -> p t w (h r e)", w=2),
                    in1=from_im[:, tiles].rearrange("p t (w h) r e -> p t w (h r e)", w=2),
                    op=ALU.add,
                )
                for which in range(2):
                    nc.sync.dma_start(
                        out=out_views[which][:, step * STEP_TILES + first : step * STEP_TILES + first + run, :],
                        in_=rotated[:, which, tiles],
                    )

        for step in range(STEPS + 2):
            next_part = step // TRIG_STEPS + 1
            build_next_part = step % TRIG_STEPS == TRIG_STEPS - 1 and next_part < TRIG_PARTS
            if step + LOADS_AHEAD < STEPS:
                load(step + LOADS_AHEAD)
            if step < STEPS:
                transpose_and_group(step)
            if build_next_part:
                sines(next_part)
            if 1 <= step <= STEPS:
                project(step - 1)
            if step >= 2:
                rotate_and_store(step - 2, pieces=STEP_BANKS if step - 2 == STEPS - 1 else 1)
            if step < STEPS:
                quantise(step)
            if build_next_part:
                cosines(next_part)
